import numpy as np
import ml_dtypes


def mxq(x, axis, fmt="e4m3"):
    dtype, down = {"e4m3": (ml_dtypes.float8_e4m3fn, 7), "e5m2": (ml_dtypes.float8_e5m2, 14)}[fmt]
    v = np.moveaxis(np.asarray(x, np.float32).astype(ml_dtypes.bfloat16).astype(np.float64), axis, -1)
    blocks = v.reshape(v.shape[:-1] + (-1, 32))
    amax = np.abs(blocks).max(-1, keepdims=True)
    byte = np.maximum(np.where(amax > 0, np.frexp(amax)[1] - 1 + 127, 0) - down, 1)
    scale = np.exp2(byte - 127.0)
    codes = (blocks / scale).astype(np.float32).astype(dtype).astype(np.float64)
    return np.moveaxis((codes * scale).reshape(v.shape), -1, axis)


WIDE = False


def mx_kscale(k):
    if not WIDE:
        return np.ones(k)
    levels = np.array([10, -10, 5, -5, 0])
    a = np.random.permutation(np.resize(levels, k // 512 * 4)).reshape(k // 512, 4)
    idx = np.arange(k)
    return np.exp2(a[idx // 512, idx % 128 // 32])


BF16 = ml_dtypes.bfloat16


def bf(x):
    return np.asarray(x, np.float32).astype(BF16)


def f64(x):
    return np.asarray(x).astype(np.float64)


BATCH, IN_Q, OUT_Q = 256, 4096, 256
K, N = 4 * IN_Q, 4 * OUT_Q


def _quat_block_matrix(W):
    Ww, Wx, Wy, Wz = W[..., 0], W[..., 1], W[..., 2], W[..., 3]
    row_w = np.stack([Ww, -Wx, -Wy, -Wz], axis=0)
    row_x = np.stack([Wx, Ww, -Wz, Wy], axis=0)
    row_y = np.stack([Wy, Wz, Ww, -Wx], axis=0)
    row_z = np.stack([Wz, -Wy, Wx, Ww], axis=0)
    return np.stack([row_w, row_x, row_y, row_z], axis=0)


def setup_inputs():
    s = mx_kscale(K)[::4]
    sigma = 1.0 / np.sqrt(2.0 * (IN_Q + OUT_Q))
    return {"x": bf(np.random.standard_normal((BATCH, IN_Q, 4)) * s[None, :, None]),
            "W": bf(np.random.standard_normal((OUT_Q, IN_Q, 4)) * sigma / s[None, :, None]),
            "B": bf(np.random.standard_normal((OUT_Q, 4)) * 0.2)}


def reference(x, W, B):
    Wq = mxq(f64(W).reshape(OUT_Q, K), 1, "e4m3").reshape(OUT_Q, IN_Q, 4)
    M = _quat_block_matrix(Wq)
    Mk = M.transpose(3, 1, 2, 0).reshape(K, N)
    xk = f64(x).reshape(BATCH, K)
    s = (mxq(xk, 1, "e4m3") @ Mk).reshape(BATCH, OUT_Q, 4)
    s = s + f64(B)
    return np.tanh(s)

@@ -1,0 +1,236 @@
+from contextlib import ExitStack
+
+import concourse.mybir as mybir
+from concourse.masks import make_identity
+
+F32 = mybir.dt.float32
+BF16 = mybir.dt.bfloat16
+U32 = mybir.dt.uint32
+U8 = mybir.dt.uint8
+FP8X4 = mybir.dt.float8_e4m3fn_x4
+ADD = mybir.AluOpType.add
+SUBTRACT = mybir.AluOpType.subtract
+MULT = mybir.AluOpType.mult
+
+P = 128
+PACK = 4
+COMPS = 4
+HALVES = 2
+ROWS = 256
+ROW_TILES = ROWS // P
+IN_Q = 4096
+GROUP_Q = P * PACK
+GROUPS = IN_Q // GROUP_Q
+GROUP_K = GROUP_Q * COMPS
+RUN = 32
+ZONES = P // RUN
+UNITS = 2 * GROUPS
+BANK = 512
+
+SIGN = ((1, -1, -1, -1), (1, 1, -1, 1), (1, 1, 1, -1), (1, -1, 1, 1))
+MAJORITY = (-1, 1, 1, 1)
+assert all(sum(SIGN[d]) == 2 * MAJORITY[d] for d in range(COMPS))
+
+LOAD_AHEAD = 5
+SORT_AHEAD = 2
+QUANTISE_BEHIND = 1
+MULTIPLY_BEHIND = 3
+
+FLOPS = 2 * ROWS * (COMPS * IN_Q) * (COMPS * ROWS)
+
+
+def tile_quatnetpytorchdenselayer_k_kernel(tc, x, W, B, out):
+    nc = tc.nc
+    operand_rows = (x.rearrange("b i c -> b (i c)"), W.rearrange("o i c -> o (i c)"))
+    out_rows = out.rearrange("b o d -> b (o d)")
+
+    with ExitStack() as ctx:
+        const = ctx.enter_context(tc.tile_pool(name="const", bufs=1))
+        keep = ctx.enter_context(tc.tile_pool(name="keep", bufs=1))
+        raw_pool = ctx.enter_context(tc.tile_pool(name="raw", bufs=ROW_TILES * (LOAD_AHEAD + 1)))
+        words_pool = ctx.enter_context(tc.tile_pool(name="words", bufs=ROW_TILES * (SORT_AHEAD + 1)))
+        grouped_pool = ctx.enter_context(tc.tile_pool(name="grouped", bufs=3))
+        last = ctx.enter_context(tc.tile_pool(name="last", bufs=ROW_TILES))
+        sums = ctx.enter_context(tc.psum_pool(name="sums", bufs=1))
+        banks = ctx.enter_context(tc.psum_pool(name="banks", bufs=4))
+        ctx.enter_context(tc.manual_schedule())
+
+        identity = const.tile([P, P], F32)
+        make_identity(nc, identity[:])
+
+        warm = const.tile([P, 1], F32)
+        nc.vector.memset(warm[:], 0.0)
+        warm_out = const.tile([P, 1], F32)
+        nc.scalar.activation(out=warm_out[:], in_=warm[:], func=mybir.ActivationFunctionType.Tanh)
+
+        codes = [
+            [keep.tile([P, COMPS * ROWS], U32, name="codes%d_%d" % (side, g), align_bytes=64) for g in range(GROUPS)]
+            for side in range(2)
+        ]
+        scales = [
+            [keep.tile([P, COMPS * ROWS], U8, name="scales%d_%d" % (side, g), align_bytes=64) for g in range(GROUPS)]
+            for side in range(2)
+        ]
+        main = [[sums.tile([P, BANK], F32, name="main%d_%d" % (bt, j)) for j in range(2)] for bt in range(ROW_TILES)]
+
+        raw = {}
+        words = {}
+        turned = {}
+        grouped = {}
+
+        def load(unit):
+            group, side = divmod(unit, 2)
+            for r in range(ROW_TILES):
+                raw[(unit, r)] = raw_pool.tile([P, GROUP_K], BF16, name="raw")
+                nc.sync.dma_start(
+                    out=raw[(unit, r)][:],
+                    in_=operand_rows[side][r * P : (r + 1) * P, group * GROUP_K : (group + 1) * GROUP_K],
+                )
+
+        def sort_words(unit):
+            for r in range(ROW_TILES):
+                words[(unit, r)] = words_pool.tile([P, HALVES, PACK, ZONES, RUN], F32, name="words")
+                nc.vector.tensor_copy(
+                    out=words[(unit, r)][:],
+                    in_=raw[(unit, r)][:]
+                    .bitcast(F32)
+                    .rearrange("p (g t q h) -> p h t g q", g=ZONES, t=PACK, q=RUN, h=HALVES),
+                )
+
+        def transpose(unit):
+            for r in range(ROW_TILES):
+                for h in range(HALVES):
+                    turned[(unit, r, h)] = banks.tile([P, PACK, P], F32, name="bank")
+                    for t in range(PACK):
+                        nc.tensor.transpose(
+                            turned[(unit, r, h)][:, t, :],
+                            words[(unit, r)][:, h, t].rearrange("p g q -> p (g q)"),
+                            identity[:],
+                        )
+
+        def regroup(unit):
+            grouped[unit] = grouped_pool.tile([P, COMPS, ROWS, PACK], BF16, name="grouped", align_bytes=64)
+            for r in range(ROW_TILES):
+                for h in range(HALVES):
+                    pairs = turned[(unit, r, h)][:].bitcast(BF16).rearrange("p t (n e) -> p e n t", e=2)
+                    target = grouped[unit][:, 2 * h : 2 * h + 2, r * P : (r + 1) * P, :]
+                    if (r, h) == (ROW_TILES - 1, HALVES - 1):
+                        nc.vector.tensor_copy(out=target, in_=pairs)
+                    else:
+                        nc.scalar.copy(out=target, in_=pairs)
+
+        def quantise(unit):
+            group, side = divmod(unit, 2)
+            nc.vector.quantize_mx(
+                out=codes[side][group][:].bitcast(FP8X4),
+                scales=scales[side][group][:],
+                in_=grouped[unit][:].rearrange("p c n t -> p (c n t)"),
+            )
+
+        def one_pass(acc, group, bt, c, d, start, stop):
+            x_cols = slice(c * ROWS + bt * P, c * ROWS + (bt + 1) * P)
+            w_cols = slice((d ^ c) * ROWS, ((d ^ c) + 1) * ROWS)
+            nc.tensor.matmul_mx(
+                out=acc,
+                lhsT=codes[0][group][:, x_cols].bitcast(FP8X4),
+                lhsT_scale=scales[0][group][:, x_cols],
+                rhs=codes[1][group][:, w_cols].bitcast(FP8X4),
+                rhs_scale=scales[1][group][:, w_cols],
+                start=start,
+                stop=stop,
+            )
+
+        def multiply_main(group, bt):
+            for j in range(2):
+                terms = [(c, d) for d in (2 * j, 2 * j + 1) for c in range(COMPS) if SIGN[d][c] == MAJORITY[d]]
+                for n, (c, d) in enumerate(terms):
+                    one_pass(
+                        main[bt][j][:, (d % 2) * ROWS : (d % 2 + 1) * ROWS],
+                        group,
+                        bt,
+                        c,
+                        d,
+                        start=(group == 0 and n == 0),
+                        stop=(group == GROUPS - 1 and n == len(terms) - 1),
+                    )
+
+        def load_bias():
+            nc.sync.dma_start(out=bias_rows[:], in_=B.rearrange("o d -> (o d)").partition_broadcast(P))
+            for d in range(COMPS):
+                nc.gpsimd.tensor_scalar(
+                    out=signed_bias[:, d, :],
+                    in0=bias_rows[:].rearrange("p (o d) -> p d o", d=COMPS)[:, d, :],
+                    scalar1=float(MAJORITY[d]),
+                    scalar2=0.0,
+                    op0=MULT,
+                    op1=ADD,
+                )
+
+        bias_rows = const.tile([P, ROWS * COMPS], BF16)
+        signed_bias = const.tile([P, COMPS, ROWS], F32)
+
+        for unit in range(LOAD_AHEAD):
+            load(unit)
+        for unit in range(SORT_AHEAD):
+            sort_words(unit)
+        for step in range(UNITS + MULTIPLY_BEHIND):
+            if step + LOAD_AHEAD < UNITS:
+                load(step + LOAD_AHEAD)
+            if step + LOAD_AHEAD == UNITS:
+                load_bias()
+            if step < UNITS:
+                transpose(step)
+            if 0 <= step - QUANTISE_BEHIND < UNITS:
+                quantise(step - QUANTISE_BEHIND)
+            if step < UNITS:
+                regroup(step)
+            if step + SORT_AHEAD < UNITS:
+                sort_words(step + SORT_AHEAD)
+            if step >= MULTIPLY_BEHIND:
+                group, bt = divmod(step - MULTIPLY_BEHIND, ROW_TILES)
+                multiply_main(group, bt)
+
+        held = []
+        for bt in range(ROW_TILES):
+            held.append(last.tile([P, COMPS, ROWS], F32, name="held"))
+            for j in range(2):
+                nc.vector.tensor_tensor(
+                    out=held[bt][:, 2 * j : 2 * j + 2, :].rearrange("p d o -> p (d o)"),
+                    in0=main[bt][j][:],
+                    in1=signed_bias[:, 2 * j : 2 * j + 2, :].rearrange("p d o -> p (d o)"),
+                    op=ADD,
+                )
+        for bt in range(ROW_TILES):
+            total = last.tile([P, COMPS, ROWS], F32, name="total")
+            for j in range(2):
+                odd = banks.tile([P, BANK], F32, name="bank")
+                for d in (2 * j, 2 * j + 1):
+                    c = [c for c in range(COMPS) if SIGN[d][c] != MAJORITY[d]][0]
+                    for group in range(GROUPS):
+                        one_pass(
+                            odd[:, (d % 2) * ROWS : (d % 2 + 1) * ROWS],
+                            group,
+                            bt,
+                            c,
+                            d,
+                            start=(group == 0),
+                            stop=(group == GROUPS - 1),
+                        )
+                for d in (2 * j, 2 * j + 1):
+                    odd_d = odd[:, (d % 2) * ROWS : (d % 2 + 1) * ROWS]
+                    if MAJORITY[d] > 0:
+                        nc.vector.tensor_tensor(out=total[:, d, :], in0=held[bt][:, d, :], in1=odd_d, op=SUBTRACT)
+                    else:
+                        nc.vector.tensor_tensor(out=total[:, d, :], in0=odd_d, in1=held[bt][:, d, :], op=SUBTRACT)
+            result = last.tile([P, ROWS, COMPS], F32, name="result")
+            for o_half in range(2):
+                o_cols = slice(o_half * P, (o_half + 1) * P)
+                nc.scalar.activation(
+                    out=result[:, o_cols, :],
+                    in_=total[:, :, o_cols].rearrange("p d o -> p o d"),
+                    func=mybir.ActivationFunctionType.Tanh,
+                )
+                nc.sync.dma_start(
+                    out=out_rows[bt * P : (bt + 1) * P, o_half * P * COMPS : (o_half + 1) * P * COMPS],
+                    in_=result[:, o_cols, :].rearrange("p o d -> p (o d)"),
+                )

@@ -34,7 +34,9 @@ assert all(sum(SIGN[d]) == 2 * MAJORITY[d] for d in range(COMPS))
 LOAD_AHEAD = 5
 SORT_AHEAD = 2
 QUANTISE_BEHIND = 1
-MULTIPLY_BEHIND = 3
+MULTIPLY_BEHIND = 2
+ODD_SPLIT = 4
+ODD_FROM = 9
 
 FLOPS = 2 * ROWS * (COMPS * IN_Q) * (COMPS * ROWS)
 
@@ -140,8 +142,9 @@ def tile_quatnetpytorchdenselayer_k_kernel(tc, x, W, B, out):
                 stop=stop,
             )
 
-        def multiply_main(group, bt):
-            for j in range(2):
+        def multiply_main(half, js):
+            group, bt = divmod(half, ROW_TILES)
+            for j in js:
                 terms = [(c, d) for d in (2 * j, 2 * j + 1) for c in range(COMPS) if SIGN[d][c] == MAJORITY[d]]
                 for n, (c, d) in enumerate(terms):
                     one_pass(
@@ -154,77 +157,103 @@ def tile_quatnetpytorchdenselayer_k_kernel(tc, x, W, B, out):
                         stop=(group == GROUPS - 1 and n == len(terms) - 1),
                     )
 
+        def multiply_odd(acc, bt, j, groups, start, stop):
+            terms = [(g, c, d) for g in groups for d in (2 * j, 2 * j + 1) for c in range(COMPS) if SIGN[d][c] != MAJORITY[d]]
+            for n, (group, c, d) in enumerate(terms):
+                one_pass(
+                    acc[:, (d % 2) * ROWS : (d % 2 + 1) * ROWS],
+                    group,
+                    bt,
+                    c,
+                    d,
+                    start=(start and n == 0),
+                    stop=(stop and n == len(terms) - 1),
+                )
+
+        def combine(out, ins, acc, bt, j):
+            if j == 0:
+                for d in (0, 1):
+                    nc.vector.tensor_tensor(
+                        out=out[:, d, :], in0=ins[:, d, :], in1=acc[:, d * ROWS : (d + 1) * ROWS], op=SUBTRACT if MAJORITY[d] > 0 else ADD
+                    )
+            else:
+                nc.vector.tensor_tensor(
+                    out=out[:, 2:4, :].rearrange("p d o -> p (d o)"), in0=ins[:, 2:4, :].rearrange("p d o -> p (d o)"), in1=acc, op=SUBTRACT
+                )
+
         def load_bias():
             nc.sync.dma_start(out=bias_rows[:], in_=B.rearrange("o d -> (o d)").partition_broadcast(P))
             for d in range(COMPS):
                 nc.gpsimd.tensor_scalar(
-                    out=signed_bias[:, d, :],
+                    out=bias[:, d, :],
                     in0=bias_rows[:].rearrange("p (o d) -> p d o", d=COMPS)[:, d, :],
-                    scalar1=float(MAJORITY[d]),
+                    scalar1=1.0,
                     scalar2=0.0,
                     op0=MULT,
                     op1=ADD,
                 )
 
         bias_rows = const.tile([P, ROWS * COMPS], BF16)
-        signed_bias = const.tile([P, COMPS, ROWS], F32)
+        bias = const.tile([P, COMPS, ROWS], F32)
+        early_odd = {}
 
         for unit in range(LOAD_AHEAD):
             load(unit)
         for unit in range(SORT_AHEAD):
             sort_words(unit)
-        for step in range(UNITS + MULTIPLY_BEHIND):
+        for step in range(UNITS):
             if step + LOAD_AHEAD < UNITS:
                 load(step + LOAD_AHEAD)
             if step + LOAD_AHEAD == UNITS:
                 load_bias()
-            if step < UNITS:
-                transpose(step)
-            if 0 <= step - QUANTISE_BEHIND < UNITS:
+            transpose(step)
+            if step >= QUANTISE_BEHIND:
                 quantise(step - QUANTISE_BEHIND)
-            if step < UNITS:
-                regroup(step)
+            regroup(step)
             if step + SORT_AHEAD < UNITS:
                 sort_words(step + SORT_AHEAD)
+            if step >= MULTIPLY_BEHIND + 1:
+                multiply_main(step - MULTIPLY_BEHIND - 1, (1,))
             if step >= MULTIPLY_BEHIND:
-                group, bt = divmod(step - MULTIPLY_BEHIND, ROW_TILES)
-                multiply_main(group, bt)
-
-        held = []
-        for bt in range(ROW_TILES):
-            held.append(last.tile([P, COMPS, ROWS], F32, name="held"))
-            for j in range(2):
-                nc.vector.tensor_tensor(
-                    out=held[bt][:, 2 * j : 2 * j + 2, :].rearrange("p d o -> p (d o)"),
-                    in0=main[bt][j][:],
-                    in1=signed_bias[:, 2 * j : 2 * j + 2, :].rearrange("p d o -> p (d o)"),
-                    op=ADD,
-                )
-        for bt in range(ROW_TILES):
-            total = last.tile([P, COMPS, ROWS], F32, name="total")
-            for j in range(2):
+                multiply_main(step - MULTIPLY_BEHIND, (0,))
+            if ODD_FROM <= step < ODD_FROM + 2 * ROW_TILES:
+                bt, j = divmod(step - ODD_FROM, 2)
                 odd = banks.tile([P, BANK], F32, name="bank")
-                for d in (2 * j, 2 * j + 1):
-                    c = [c for c in range(COMPS) if SIGN[d][c] != MAJORITY[d]][0]
-                    for group in range(GROUPS):
-                        one_pass(
-                            odd[:, (d % 2) * ROWS : (d % 2 + 1) * ROWS],
-                            group,
-                            bt,
-                            c,
-                            d,
-                            start=(group == 0),
-                            stop=(group == GROUPS - 1),
-                        )
-                for d in (2 * j, 2 * j + 1):
-                    odd_d = odd[:, (d % 2) * ROWS : (d % 2 + 1) * ROWS]
-                    if MAJORITY[d] > 0:
-                        nc.vector.tensor_tensor(out=total[:, d, :], in0=held[bt][:, d, :], in1=odd_d, op=SUBTRACT)
-                    else:
-                        nc.vector.tensor_tensor(out=total[:, d, :], in0=odd_d, in1=held[bt][:, d, :], op=SUBTRACT)
+                multiply_odd(odd, bt, j, range(ODD_SPLIT), True, True)
+                early_odd[(bt, j)] = last.tile([P, BANK], F32, name="early_odd%d%d" % (bt, j), bufs=1)
+                nc.scalar.copy(out=early_odd[(bt, j)][:], in_=odd[:])
+
+        rest = [last.tile([P, COMPS, ROWS], F32, name="rest%d" % bt, bufs=1) for bt in range(ROW_TILES)]
+        quantise(UNITS - 1)
+        multiply_main(2 * GROUPS - 3, (1,))
+        odds = {}
+        for bt in range(ROW_TILES):
+            for j in range(2):
+                odds[(bt, j)] = banks.tile([P, BANK], F32, name="bank")
+                multiply_odd(odds[(bt, j)], bt, j, range(ODD_SPLIT, GROUPS - 1), True, False)
+                combine(rest[bt], bias, early_odd[(bt, j)][:], bt, j)
+        for bt in range(ROW_TILES):
+            for j in range(2):
+                multiply_odd(odds[(bt, j)], bt, j, (GROUPS - 1,), False, True)
+                combine(rest[bt], rest[bt], odds[(bt, j)][:], bt, j)
+            multiply_main(2 * (GROUPS - 1) + bt, (0, 1))
+            total = last.tile([P, COMPS, ROWS], F32, name="total")
+            for d in (0, 1):
+                nc.vector.tensor_tensor(
+                    out=total[:, d, :],
+                    in0=rest[bt][:, d, :],
+                    in1=main[bt][0][:, d * ROWS : (d + 1) * ROWS],
+                    op=ADD if MAJORITY[d] > 0 else SUBTRACT,
+                )
             result = last.tile([P, ROWS, COMPS], F32, name="result")
             for o_half in range(2):
                 o_cols = slice(o_half * P, (o_half + 1) * P)
+                nc.vector.tensor_tensor(
+                    out=total[:, 2:4, o_cols],
+                    in0=rest[bt][:, 2:4, o_cols],
+                    in1=main[bt][1][:].rearrange("p (d o) -> p d o", d=2)[:, :, o_cols],
+                    op=ADD,
+                )
                 nc.scalar.activation(
                     out=result[:, o_cols, :],
                     in_=total[:, :, o_cols].rearrange("p d o -> p o d"),

@@ -66,11 +66,11 @@ def tile_quatnetpytorchdenselayer_k_kernel(tc, x, W, B, out):
         nc.scalar.activation(out=warm_out[:], in_=warm[:], func=mybir.ActivationFunctionType.Tanh)
 
         codes = [
-            [keep.tile([P, COMPS * ROWS], U32, name="codes%d_%d" % (side, g), align_bytes=64) for g in range(GROUPS)]
+            [keep.tile([P, COMPS * ROWS], U32, name="codes%d_%d" % (side, g), align_bytes=256) for g in range(GROUPS)]
             for side in range(2)
         ]
         scales = [
-            [keep.tile([P, COMPS * ROWS], U8, name="scales%d_%d" % (side, g), align_bytes=64) for g in range(GROUPS)]
+            [keep.tile([P, COMPS * ROWS], U8, name="scales%d_%d" % (side, g), align_bytes=256) for g in range(GROUPS)]
             for side in range(2)
         ]
         main = [[sums.tile([P, BANK], F32, name="main%d_%d" % (bt, j)) for j in range(2)] for bt in range(ROW_TILES)]

@@ -35,8 +35,16 @@ LOAD_AHEAD = 5
 SORT_AHEAD = 2
 QUANTISE_BEHIND = 1
 MULTIPLY_BEHIND = 2
-ODD_SPLIT = 4
-ODD_FROM = 9
+ODD_SPLIT = 3
+ODD_STEPS = (7, 9, 11, 13)
+ODD_ON_SCALAR = 1
+V_BANK = (1, 1)
+S_PERIOD = 2
+S_PHASE = 1
+V_ORDER = "QSX"
+V_HEAD = "QXS"
+HEAD = 4
+QUOTAS = (4, 4, 2, 4, 4, 5)
 
 FLOPS = 2 * ROWS * (COMPS * IN_Q) * (COMPS * ROWS)
 
@@ -116,7 +124,7 @@ def tile_quatnetpytorchdenselayer_k_kernel(tc, x, W, B, out):
                 for h in range(HALVES):
                     pairs = turned[(unit, r, h)][:].bitcast(BF16).rearrange("p t (n e) -> p e n t", e=2)
                     target = grouped[unit][:, 2 * h : 2 * h + 2, r * P : (r + 1) * P, :]
-                    if (r, h) == (ROW_TILES - 1, HALVES - 1):
+                    if (r, h) == V_BANK and unit % S_PERIOD != S_PHASE:
                         nc.vector.tensor_copy(out=target, in_=pairs)
                     else:
                         nc.scalar.copy(out=target, in_=pairs)
@@ -142,20 +150,19 @@ def tile_quatnetpytorchdenselayer_k_kernel(tc, x, W, B, out):
                 stop=stop,
             )
 
-        def multiply_main(half, js):
+        def multiply_main(half, d):
             group, bt = divmod(half, ROW_TILES)
-            for j in js:
-                terms = [(c, d) for d in (2 * j, 2 * j + 1) for c in range(COMPS) if SIGN[d][c] == MAJORITY[d]]
-                for n, (c, d) in enumerate(terms):
-                    one_pass(
-                        main[bt][j][:, (d % 2) * ROWS : (d % 2 + 1) * ROWS],
-                        group,
-                        bt,
-                        c,
-                        d,
-                        start=(group == 0 and n == 0),
-                        stop=(group == GROUPS - 1 and n == len(terms) - 1),
-                    )
+            terms = [c for c in range(COMPS) if SIGN[d][c] == MAJORITY[d]]
+            for n, c in enumerate(terms):
+                one_pass(
+                    main[bt][d // 2][:, (d % 2) * ROWS : (d % 2 + 1) * ROWS],
+                    group,
+                    bt,
+                    c,
+                    d,
+                    start=(group == 0 and d % 2 == 0 and n == 0),
+                    stop=(group == GROUPS - 1 and d % 2 == 1 and n == len(terms) - 1),
+                )
 
         def multiply_odd(acc, bt, j, groups, start, stop):
             terms = [(g, c, d) for g in groups for d in (2 * j, 2 * j + 1) for c in range(COMPS) if SIGN[d][c] != MAJORITY[d]]
@@ -201,31 +208,38 @@ def tile_quatnetpytorchdenselayer_k_kernel(tc, x, W, B, out):
             load(unit)
         for unit in range(SORT_AHEAD):
             sort_words(unit)
+        waiting = []
+        odd_items = [(bt, j) for bt in range(ROW_TILES) for j in range(2)]
         for step in range(UNITS):
             if step + LOAD_AHEAD < UNITS:
                 load(step + LOAD_AHEAD)
             if step + LOAD_AHEAD == UNITS:
                 load_bias()
             transpose(step)
-            if step >= QUANTISE_BEHIND:
-                quantise(step - QUANTISE_BEHIND)
-            regroup(step)
-            if step + SORT_AHEAD < UNITS:
-                sort_words(step + SORT_AHEAD)
-            if step >= MULTIPLY_BEHIND + 1:
-                multiply_main(step - MULTIPLY_BEHIND - 1, (1,))
-            if step >= MULTIPLY_BEHIND:
-                multiply_main(step - MULTIPLY_BEHIND, (0,))
-            if ODD_FROM <= step < ODD_FROM + 2 * ROW_TILES:
-                bt, j = divmod(step - ODD_FROM, 2)
+            for stage in V_ORDER if step >= HEAD else V_HEAD:
+                if stage == "Q" and step >= 1:
+                    quantise(step - 1)
+                    if step % 2 == 0:
+                        waiting += [(step - 2 + bt, d) for bt in range(ROW_TILES) for d in range(COMPS)]
+                if stage == "X":
+                    regroup(step)
+                if stage == "S" and step + SORT_AHEAD < UNITS:
+                    sort_words(step + SORT_AHEAD)
+            quota = QUOTAS[min(step, len(QUOTAS) - 1)]
+            for half, d in waiting[:quota]:
+                multiply_main(half, d)
+            waiting = waiting[quota:]
+            if step in ODD_STEPS and odd_items:
+                bt, j = odd_items.pop(0)
                 odd = banks.tile([P, BANK], F32, name="bank")
                 multiply_odd(odd, bt, j, range(ODD_SPLIT), True, True)
                 early_odd[(bt, j)] = last.tile([P, BANK], F32, name="early_odd%d%d" % (bt, j), bufs=1)
-                nc.scalar.copy(out=early_odd[(bt, j)][:], in_=odd[:])
+                (nc.scalar.copy if ODD_ON_SCALAR else nc.vector.tensor_copy)(out=early_odd[(bt, j)][:], in_=odd[:])
 
         rest = [last.tile([P, COMPS, ROWS], F32, name="rest%d" % bt, bufs=1) for bt in range(ROW_TILES)]
         quantise(UNITS - 1)
-        multiply_main(2 * GROUPS - 3, (1,))
+        for half, d in waiting:
+            multiply_main(half, d)
         odds = {}
         for bt in range(ROW_TILES):
             for j in range(2):
@@ -236,7 +250,8 @@ def tile_quatnetpytorchdenselayer_k_kernel(tc, x, W, B, out):
             for j in range(2):
                 multiply_odd(odds[(bt, j)], bt, j, (GROUPS - 1,), False, True)
                 combine(rest[bt], rest[bt], odds[(bt, j)][:], bt, j)
-            multiply_main(2 * (GROUPS - 1) + bt, (0, 1))
+            for d in range(COMPS):
+                multiply_main(2 * (GROUPS - 1) + bt, d)
             total = last.tile([P, COMPS, ROWS], F32, name="total")
             for d in (0, 1):
                 nc.vector.tensor_tensor(

@@ -38,12 +38,18 @@ MULTIPLY_BEHIND = 2
 ODD_SPLIT = 3
 ODD_STEPS = (7, 9, 11, 13)
 ODD_ON_SCALAR = 1
-V_BANK = (1, 1)
-S_PERIOD = 2
+V_BANK = (1, 0)
+S_PERIOD = 99
 S_PHASE = 1
-V_ORDER = "QSX"
+V_ORDER = "QXS"
 V_HEAD = "QXS"
-HEAD = 4
+HEAD = 2
+HOLDS = (2,)
+DUMMIES = ()
+FIRST_PIECES = 2
+FIRST_UNITS = 1
+TAIL_PIECES = (2, 4)
+ON_GPSIMD = ()
 QUOTAS = (4, 4, 2, 4, 4, 5)
 
 FLOPS = 2 * ROWS * (COMPS * IN_Q) * (COMPS * ROWS)
@@ -68,6 +74,9 @@ def tile_quatnetpytorchdenselayer_k_kernel(tc, x, W, B, out):
         identity = const.tile([P, P], F32)
         make_identity(nc, identity[:])
 
+        warm_rows = const.tile([P, P + BANK], BF16)
+        nc.gpsimd.memset(warm_rows[:], 0.0)
+
         warm = const.tile([P, 1], F32)
         nc.vector.memset(warm[:], 0.0)
         warm_out = const.tile([P, 1], F32)
@@ -88,24 +97,31 @@ def tile_quatnetpytorchdenselayer_k_kernel(tc, x, W, B, out):
         turned = {}
         grouped = {}
 
+        def pieces_of(unit):
+            return FIRST_PIECES if unit < FIRST_UNITS else 1
+
         def load(unit):
             group, side = divmod(unit, 2)
             for r in range(ROW_TILES):
                 raw[(unit, r)] = raw_pool.tile([P, GROUP_K], BF16, name="raw")
-                nc.sync.dma_start(
-                    out=raw[(unit, r)][:],
-                    in_=operand_rows[side][r * P : (r + 1) * P, group * GROUP_K : (group + 1) * GROUP_K],
-                )
+                parts = pieces_of(unit)
+                for n in range(parts):
+                    cols = slice(n * GROUP_K // parts, (n + 1) * GROUP_K // parts)
+                    nc.sync.dma_start(
+                        out=raw[(unit, r)][:, cols],
+                        in_=operand_rows[side][r * P : (r + 1) * P, group * GROUP_K + cols.start : group * GROUP_K + cols.stop],
+                    )
 
         def sort_words(unit):
             for r in range(ROW_TILES):
                 words[(unit, r)] = words_pool.tile([P, HALVES, PACK, ZONES, RUN], F32, name="words")
-                nc.vector.tensor_copy(
-                    out=words[(unit, r)][:],
-                    in_=raw[(unit, r)][:]
-                    .bitcast(F32)
-                    .rearrange("p (g t q h) -> p h t g q", g=ZONES, t=PACK, q=RUN, h=HALVES),
-                )
+                source = raw[(unit, r)][:].bitcast(F32).rearrange("p (g t q h) -> p h t g q", g=ZONES, t=PACK, q=RUN, h=HALVES)
+                parts = pieces_of(unit)
+                for n in range(parts):
+                    zones = slice(n * ZONES // parts, (n + 1) * ZONES // parts)
+                    (nc.gpsimd if (unit, r) in ON_GPSIMD else nc.vector).tensor_copy(
+                        out=words[(unit, r)][:, :, :, zones], in_=source[:, :, :, zones]
+                    )
 
         def transpose(unit):
             for r in range(ROW_TILES):
@@ -225,7 +241,10 @@ def tile_quatnetpytorchdenselayer_k_kernel(tc, x, W, B, out):
                     regroup(step)
                 if stage == "S" and step + SORT_AHEAD < UNITS:
                     sort_words(step + SORT_AHEAD)
+            for n in range(DUMMIES[step] if step < len(DUMMIES) else 0):
+                nc.tensor.matmul(main[1][1][:], lhsT=warm_rows[:, :P], rhs=warm_rows[:, P:], start=True, stop=True)
             quota = QUOTAS[min(step, len(QUOTAS) - 1)]
+            quota = min(quota, max(0, len(waiting) - HOLDS[min(step, len(HOLDS) - 1)]))
             for half, d in waiting[:quota]:
                 multiply_main(half, d)
             waiting = waiting[quota:]
@@ -261,8 +280,9 @@ def tile_quatnetpytorchdenselayer_k_kernel(tc, x, W, B, out):
                     op=ADD if MAJORITY[d] > 0 else SUBTRACT,
                 )
             result = last.tile([P, ROWS, COMPS], F32, name="result")
-            for o_half in range(2):
-                o_cols = slice(o_half * P, (o_half + 1) * P)
+            parts = TAIL_PIECES[bt]
+            for o_part in range(parts):
+                o_cols = slice(o_part * ROWS // parts, (o_part + 1) * ROWS // parts)
                 nc.vector.tensor_tensor(
                     out=total[:, 2:4, o_cols],
                     in0=rest[bt][:, 2:4, o_cols],
@@ -275,6 +295,6 @@ def tile_quatnetpytorchdenselayer_k_kernel(tc, x, W, B, out):
                     func=mybir.ActivationFunctionType.Tanh,
                 )
                 nc.sync.dma_start(
-                    out=out_rows[bt * P : (bt + 1) * P, o_half * P * COMPS : (o_half + 1) * P * COMPS],
+                    out=out_rows[bt * P : (bt + 1) * P, o_cols.start * COMPS : o_cols.stop * COMPS],
                     in_=result[:, o_cols, :].rearrange("p o d -> p (o d)"),
                 )

@@ -39,18 +39,34 @@ ODD_SPLIT = 3
 ODD_STEPS = (7, 9, 11, 13)
 ODD_ON_SCALAR = 1
 V_BANK = (1, 0)
-S_PERIOD = 99
-S_PHASE = 1
-V_ORDER = "QXS"
-V_HEAD = "QXS"
-HEAD = 2
-HOLDS = (2,)
+S_UNITS = ()
+V_ORDER = "QXSTP"
+V_HEAD = "QXASTP"
+HEAD = 3
+HOLDS = (6, 2) * 8
+TURNED_FROM = 15
+PAIRS = PACK // 2
+BLOCK = 32
+BLOCK_ROWS = BLOCK // PAIRS
+BY_GPSIMD = 4
+SPLIT_PIECES = 2
+SPLIT_BUFS = 4
+TURN_LOADS = (5,)
+WIDE_BUFS = 1
+SPLIT_QUOTA = 1
+SPLIT_STEPS = (7, 9, 11, 13)
+TURN_STEPS = (13, 14)
+TURN_QUOTA = 2
+LAST_Q = 0
+SPLIT_FROM = 99
+SPLIT_TO = 99
+BANK_ORDER = ((0, 0), (0, 1), (1, 0), (1, 1))
 DUMMIES = ()
 FIRST_PIECES = 2
 FIRST_UNITS = 1
 TAIL_PIECES = (2, 4)
-ON_GPSIMD = ()
-QUOTAS = (4, 4, 2, 4, 4, 5)
+ON_GPSIMD = ((2, 1), (3, 1), (4, 1))
+QUOTAS = (4, 4, 2, 4, 4, 4, 4, 4, 4, 5)
 
 FLOPS = 2 * ROWS * (COMPS * IN_Q) * (COMPS * ROWS)
 
@@ -66,6 +82,9 @@ def tile_quatnetpytorchdenselayer_k_kernel(tc, x, W, B, out):
         raw_pool = ctx.enter_context(tc.tile_pool(name="raw", bufs=ROW_TILES * (LOAD_AHEAD + 1)))
         words_pool = ctx.enter_context(tc.tile_pool(name="words", bufs=ROW_TILES * (SORT_AHEAD + 1)))
         grouped_pool = ctx.enter_context(tc.tile_pool(name="grouped", bufs=3))
+        wide_pool = ctx.enter_context(tc.tile_pool(name="wide", bufs=WIDE_BUFS))
+        split_pool = ctx.enter_context(tc.tile_pool(name="split", bufs=SPLIT_BUFS))
+        turned_pool = ctx.enter_context(tc.tile_pool(name="turned", bufs=1))
         last = ctx.enter_context(tc.tile_pool(name="last", bufs=ROW_TILES))
         sums = ctx.enter_context(tc.psum_pool(name="sums", bufs=1))
         banks = ctx.enter_context(tc.psum_pool(name="banks", bufs=4))
@@ -73,9 +92,6 @@ def tile_quatnetpytorchdenselayer_k_kernel(tc, x, W, B, out):
 
         identity = const.tile([P, P], F32)
         make_identity(nc, identity[:])
-
-        warm_rows = const.tile([P, P + BANK], BF16)
-        nc.gpsimd.memset(warm_rows[:], 0.0)
 
         warm = const.tile([P, 1], F32)
         nc.vector.memset(warm[:], 0.0)
@@ -100,7 +116,38 @@ def tile_quatnetpytorchdenselayer_k_kernel(tc, x, W, B, out):
         def pieces_of(unit):
             return FIRST_PIECES if unit < FIRST_UNITS else 1
 
+        def load_turned(unit):
+            group, side = divmod(unit, 2)
+            raw[unit] = wide_pool.tile([P, ROWS // BLOCK_ROWS, GROUP_K // ZONES // PAIRS], BF16, name="wide")
+            source = operand_rows[side][:, group * GROUP_K : (group + 1) * GROUP_K].rearrange(
+                "(n r) (z u k) -> z u r n k", r=BLOCK_ROWS, z=ZONES, u=PAIRS
+            )
+            for z in range(ZONES):
+                for u in range(PAIRS):
+                    nc.sync.dma_start(out=raw[unit][BLOCK * z + u : BLOCK * (z + 1) : PAIRS], in_=source[z, u])
+
+        def split(unit, c):
+            words[(unit, c)] = split_pool.tile([P, ROWS // BLOCK_ROWS, BLOCK, 2], BF16, name="split", align_bytes=64)
+            source = raw[unit][:].rearrange("p n (e q c) -> p c n q e", e=2, q=BLOCK)[:, c]
+            if c < BY_GPSIMD:
+                for n in range(SPLIT_PIECES):
+                    rows = slice(n * 16 // SPLIT_PIECES, (n + 1) * 16 // SPLIT_PIECES)
+                    nc.gpsimd.tensor_scalar(out=words[(unit, c)][:, rows], in0=source[:, rows], scalar1=1.0, scalar2=0.0, op0=MULT, op1=ADD)
+            else:
+                nc.vector.tensor_copy(out=words[(unit, c)][:], in_=source)
+
+        def turn(unit, c):
+            if c == 0:
+                grouped[unit] = turned_pool.tile([P, COMPS, ROWS, PACK], BF16, name="turned", align_bytes=64)
+            nc.vector.transpose(
+                grouped[unit][:, c].rearrange("p n t -> p (n t)").bitcast(F32),
+                words[(unit, c)][:].rearrange("p n q e -> p (n q e)").bitcast(F32),
+            )
+
         def load(unit):
+            if unit >= TURNED_FROM:
+                load_turned(unit)
+                return
             group, side = divmod(unit, 2)
             for r in range(ROW_TILES):
                 raw[(unit, r)] = raw_pool.tile([P, GROUP_K], BF16, name="raw")
@@ -124,8 +171,8 @@ def tile_quatnetpytorchdenselayer_k_kernel(tc, x, W, B, out):
                     )
 
         def transpose(unit):
-            for r in range(ROW_TILES):
-                for h in range(HALVES):
+            for r, h in BANK_ORDER if unit else [(r, h) for r in range(ROW_TILES) for h in range(HALVES)]:
+                if True:
                     turned[(unit, r, h)] = banks.tile([P, PACK, P], F32, name="bank")
                     for t in range(PACK):
                         nc.tensor.transpose(
@@ -136,21 +183,27 @@ def tile_quatnetpytorchdenselayer_k_kernel(tc, x, W, B, out):
 
         def regroup(unit):
             grouped[unit] = grouped_pool.tile([P, COMPS, ROWS, PACK], BF16, name="grouped", align_bytes=64)
-            for r in range(ROW_TILES):
-                for h in range(HALVES):
+            for r, h in BANK_ORDER if unit else [(r, h) for r in range(ROW_TILES) for h in range(HALVES)]:
+                if True:
                     pairs = turned[(unit, r, h)][:].bitcast(BF16).rearrange("p t (n e) -> p e n t", e=2)
                     target = grouped[unit][:, 2 * h : 2 * h + 2, r * P : (r + 1) * P, :]
-                    if (r, h) == V_BANK and unit % S_PERIOD != S_PHASE:
+                    if (r, h) == V_BANK and unit not in S_UNITS:
                         nc.vector.tensor_copy(out=target, in_=pairs)
                     else:
                         nc.scalar.copy(out=target, in_=pairs)
 
-        def quantise(unit):
+        def quantise(unit, parts=(0, 1)):
             group, side = divmod(unit, 2)
+            if parts == (0, 1):
+                cols = slice(0, COMPS * ROWS)
+                source = grouped[unit][:]
+            else:
+                cols = slice(parts[0] * 2 * ROWS, (parts[0] + 1) * 2 * ROWS)
+                source = grouped[unit][:, 2 * parts[0] : 2 * parts[0] + 2]
             nc.vector.quantize_mx(
-                out=codes[side][group][:].bitcast(FP8X4),
-                scales=scales[side][group][:],
-                in_=grouped[unit][:].rearrange("p c n t -> p (c n t)"),
+                out=codes[side][group][:, cols].bitcast(FP8X4),
+                scales=scales[side][group][:, cols],
+                in_=source.rearrange("p c n t -> p (c n t)"),
             )
 
         def one_pass(acc, group, bt, c, d, start, stop):
@@ -193,16 +246,13 @@ def tile_quatnetpytorchdenselayer_k_kernel(tc, x, W, B, out):
                     stop=(stop and n == len(terms) - 1),
                 )
 
-        def combine(out, ins, acc, bt, j):
+        def combine(out, ins, acc, j):
             if j == 0:
                 for d in (0, 1):
-                    nc.vector.tensor_tensor(
-                        out=out[:, d, :], in0=ins[:, d, :], in1=acc[:, d * ROWS : (d + 1) * ROWS], op=SUBTRACT if MAJORITY[d] > 0 else ADD
-                    )
+                    cols = slice(d * ROWS, (d + 1) * ROWS)
+                    nc.vector.tensor_tensor(out=out[:, cols], in0=ins[:, cols], in1=acc[:, cols], op=SUBTRACT if MAJORITY[d] > 0 else ADD)
             else:
-                nc.vector.tensor_tensor(
-                    out=out[:, 2:4, :].rearrange("p d o -> p (d o)"), in0=ins[:, 2:4, :].rearrange("p d o -> p (d o)"), in1=acc, op=SUBTRACT
-                )
+                nc.vector.tensor_tensor(out=out, in0=ins, in1=acc, op=SUBTRACT)
 
         def load_bias():
             nc.sync.dma_start(out=bias_rows[:], in_=B.rearrange("o d -> (o d)").partition_broadcast(P))
@@ -226,23 +276,39 @@ def tile_quatnetpytorchdenselayer_k_kernel(tc, x, W, B, out):
             sort_words(unit)
         waiting = []
         odd_items = [(bt, j) for bt in range(ROW_TILES) for j in range(2)]
-        for step in range(UNITS):
-            if step + LOAD_AHEAD < UNITS:
+        splits = [(u, c) for u in range(TURNED_FROM, UNITS) for c in range(COMPS)]
+        turns = list(splits)
+        done_early = []
+        for step in range(TURNED_FROM):
+            if step + LOAD_AHEAD < TURNED_FROM:
                 load(step + LOAD_AHEAD)
-            if step + LOAD_AHEAD == UNITS:
+            if step in TURN_LOADS:
+                load_turned(TURNED_FROM + TURN_LOADS.index(step))
+            if step == 11:
                 load_bias()
             transpose(step)
             for stage in V_ORDER if step >= HEAD else V_HEAD:
                 if stage == "Q" and step >= 1:
-                    quantise(step - 1)
+                    quantise(step - 1, (1,) if step - 1 >= SPLIT_FROM and step - 1 < SPLIT_TO else (0, 1))
                     if step % 2 == 0:
                         waiting += [(step - 2 + bt, d) for bt in range(ROW_TILES) for d in range(COMPS)]
                 if stage == "X":
                     regroup(step)
-                if stage == "S" and step + SORT_AHEAD < UNITS:
+                if stage == "A" and SPLIT_FROM <= step < SPLIT_TO:
+                    quantise(step, (0,))
+                if stage == "T" and step in TURN_STEPS:
+                    for u, c in turns[:TURN_QUOTA]:
+                        if c == 0 and u > TURNED_FROM:
+                            quantise(u - 1)
+                            done_early.append(u - 1)
+                        turn(u, c)
+                    turns = turns[TURN_QUOTA:]
+                if stage == "P" and step in SPLIT_STEPS:
+                    for u, c in splits[:SPLIT_QUOTA]:
+                        split(u, c)
+                    splits = splits[SPLIT_QUOTA:]
+                if stage == "S" and step + SORT_AHEAD < TURNED_FROM:
                     sort_words(step + SORT_AHEAD)
-            for n in range(DUMMIES[step] if step < len(DUMMIES) else 0):
-                nc.tensor.matmul(main[1][1][:], lhsT=warm_rows[:, :P], rhs=warm_rows[:, P:], start=True, stop=True)
             quota = QUOTAS[min(step, len(QUOTAS) - 1)]
             quota = min(quota, max(0, len(waiting) - HOLDS[min(step, len(HOLDS) - 1)]))
             for half, d in waiting[:quota]:
@@ -255,8 +321,25 @@ def tile_quatnetpytorchdenselayer_k_kernel(tc, x, W, B, out):
                 early_odd[(bt, j)] = last.tile([P, BANK], F32, name="early_odd%d%d" % (bt, j), bufs=1)
                 (nc.scalar.copy if ODD_ON_SCALAR else nc.vector.tensor_copy)(out=early_odd[(bt, j)][:], in_=odd[:])
 
-        rest = [last.tile([P, COMPS, ROWS], F32, name="rest%d" % bt, bufs=1) for bt in range(ROW_TILES)]
-        quantise(UNITS - 1)
+        if TURNED_FROM % 2:
+            quantise(TURNED_FROM - 1)
+        else:
+            quantise(TURNED_FROM - 1)
+            if TURNED_FROM < UNITS:
+                waiting += [(TURNED_FROM - 2 + bt, d) for bt in range(ROW_TILES) for d in range(COMPS)]
+        for u in range(TURNED_FROM, UNITS):
+            for c in range(COMPS):
+                if (u, c) in splits:
+                    split(u, c)
+            for c in range(COMPS):
+                if (u, c) in turns:
+                    if c == 0 and u > TURNED_FROM and u - 1 not in done_early:
+                        quantise(u - 1)
+                        done_early.append(u - 1)
+                    turn(u, c)
+        for u in range(TURNED_FROM, UNITS):
+            if u not in done_early:
+                quantise(u)
         for half, d in waiting:
             multiply_main(half, d)
         odds = {}
@@ -264,18 +347,20 @@ def tile_quatnetpytorchdenselayer_k_kernel(tc, x, W, B, out):
             for j in range(2):
                 odds[(bt, j)] = banks.tile([P, BANK], F32, name="bank")
                 multiply_odd(odds[(bt, j)], bt, j, range(ODD_SPLIT, GROUPS - 1), True, False)
-                combine(rest[bt], bias, early_odd[(bt, j)][:], bt, j)
+                rest = early_odd[(bt, j)][:]
+                combine(rest, bias[:, 2 * j : 2 * j + 2, :].rearrange("p d o -> p (d o)"), rest, j)
         for bt in range(ROW_TILES):
             for j in range(2):
                 multiply_odd(odds[(bt, j)], bt, j, (GROUPS - 1,), False, True)
-                combine(rest[bt], rest[bt], odds[(bt, j)][:], bt, j)
+                rest = early_odd[(bt, j)][:]
+                combine(rest, rest, odds[(bt, j)][:], j)
             for d in range(COMPS):
                 multiply_main(2 * (GROUPS - 1) + bt, d)
             total = last.tile([P, COMPS, ROWS], F32, name="total")
             for d in (0, 1):
                 nc.vector.tensor_tensor(
                     out=total[:, d, :],
-                    in0=rest[bt][:, d, :],
+                    in0=early_odd[(bt, 0)][:, d * ROWS : (d + 1) * ROWS],
                     in1=main[bt][0][:, d * ROWS : (d + 1) * ROWS],
                     op=ADD if MAJORITY[d] > 0 else SUBTRACT,
                 )
@@ -285,7 +370,7 @@ def tile_quatnetpytorchdenselayer_k_kernel(tc, x, W, B, out):
                 o_cols = slice(o_part * ROWS // parts, (o_part + 1) * ROWS // parts)
                 nc.vector.tensor_tensor(
                     out=total[:, 2:4, o_cols],
-                    in0=rest[bt][:, 2:4, o_cols],
+                    in0=early_odd[(bt, 1)][:].rearrange("p (d o) -> p d o", d=2)[:, :, o_cols],
                     in1=main[bt][1][:].rearrange("p (d o) -> p d o", d=2)[:, :, o_cols],
                     op=ADD,
                 )

from contextlib import ExitStack

import concourse.mybir as mybir
from concourse.masks import make_identity

F32 = mybir.dt.float32
BF16 = mybir.dt.bfloat16
U32 = mybir.dt.uint32
U8 = mybir.dt.uint8
FP8X4 = mybir.dt.float8_e4m3fn_x4
ADD = mybir.AluOpType.add
SUBTRACT = mybir.AluOpType.subtract
MULT = mybir.AluOpType.mult

P = 128
PACK = 4
COMPS = 4
HALVES = 2
ROWS = 256
ROW_TILES = ROWS // P
IN_Q = 4096
GROUP_Q = P * PACK
GROUPS = IN_Q // GROUP_Q
GROUP_K = GROUP_Q * COMPS
RUN = 32
ZONES = P // RUN
UNITS = 2 * GROUPS
BANK = 512

SIGN = ((1, -1, -1, -1), (1, 1, -1, 1), (1, 1, 1, -1), (1, -1, 1, 1))
MAJORITY = (-1, 1, 1, 1)
assert all(sum(SIGN[d]) == 2 * MAJORITY[d] for d in range(COMPS))

LOAD_AHEAD = 5
SORT_AHEAD = 2
QUANTISE_BEHIND = 1
MULTIPLY_BEHIND = 2
ODD_SPLIT = 3
ODD_STEPS = (7, 9, 11, 13)
ODD_ON_SCALAR = 1
V_BANK = (1, 0)
S_UNITS = ()
V_ORDER = "QXSTP"
V_HEAD = "QXASTP"
HEAD = 3
HOLDS = (6, 2) * 8
TURNED_FROM = 15
PAIRS = PACK // 2
BLOCK = 32
BLOCK_ROWS = BLOCK // PAIRS
BY_GPSIMD = 4
SPLIT_PIECES = 2
SPLIT_BUFS = 4
TURN_LOADS = (5,)
WIDE_BUFS = 1
SPLIT_QUOTA = 1
SPLIT_STEPS = (7, 9, 11, 13)
TURN_STEPS = (13, 14)
TURN_QUOTA = 2
LAST_Q = 0
SPLIT_FROM = 99
SPLIT_TO = 99
BANK_ORDER = ((0, 0), (0, 1), (1, 0), (1, 1))
DUMMIES = ()
FIRST_PIECES = 2
FIRST_UNITS = 1
TAIL_PIECES = (2, 4)
ON_GPSIMD = ((2, 1), (3, 1), (4, 1))
QUOTAS = (4, 4, 2, 4, 4, 4, 4, 4, 4, 5)

FLOPS = 2 * ROWS * (COMPS * IN_Q) * (COMPS * ROWS)


def tile_quatnetpytorchdenselayer_k_kernel(tc, x, W, B, out):
    nc = tc.nc
    operand_rows = (x.rearrange("b i c -> b (i c)"), W.rearrange("o i c -> o (i c)"))
    out_rows = out.rearrange("b o d -> b (o d)")

    with ExitStack() as ctx:
        const = ctx.enter_context(tc.tile_pool(name="const", bufs=1))
        keep = ctx.enter_context(tc.tile_pool(name="keep", bufs=1))
        raw_pool = ctx.enter_context(tc.tile_pool(name="raw", bufs=ROW_TILES * (LOAD_AHEAD + 1)))
        words_pool = ctx.enter_context(tc.tile_pool(name="words", bufs=ROW_TILES * (SORT_AHEAD + 1)))
        grouped_pool = ctx.enter_context(tc.tile_pool(name="grouped", bufs=3))
        wide_pool = ctx.enter_context(tc.tile_pool(name="wide", bufs=WIDE_BUFS))
        split_pool = ctx.enter_context(tc.tile_pool(name="split", bufs=SPLIT_BUFS))
        turned_pool = ctx.enter_context(tc.tile_pool(name="turned", bufs=1))
        last = ctx.enter_context(tc.tile_pool(name="last", bufs=ROW_TILES))
        sums = ctx.enter_context(tc.psum_pool(name="sums", bufs=1))
        banks = ctx.enter_context(tc.psum_pool(name="banks", bufs=4))
        ctx.enter_context(tc.manual_schedule())

        identity = const.tile([P, P], F32)
        make_identity(nc, identity[:])

        warm = const.tile([P, 1], F32)
        nc.vector.memset(warm[:], 0.0)
        warm_out = const.tile([P, 1], F32)
        nc.scalar.activation(out=warm_out[:], in_=warm[:], func=mybir.ActivationFunctionType.Tanh)

        codes = [
            [keep.tile([P, COMPS * ROWS], U32, name="codes%d_%d" % (side, g), align_bytes=256) for g in range(GROUPS)]
            for side in range(2)
        ]
        scales = [
            [keep.tile([P, COMPS * ROWS], U8, name="scales%d_%d" % (side, g), align_bytes=256) for g in range(GROUPS)]
            for side in range(2)
        ]
        main = [[sums.tile([P, BANK], F32, name="main%d_%d" % (bt, j)) for j in range(2)] for bt in range(ROW_TILES)]

        raw = {}
        words = {}
        turned = {}
        grouped = {}

        def pieces_of(unit):
            return FIRST_PIECES if unit < FIRST_UNITS else 1

        def load_turned(unit):
            group, side = divmod(unit, 2)
            raw[unit] = wide_pool.tile([P, ROWS // BLOCK_ROWS, GROUP_K // ZONES // PAIRS], BF16, name="wide")
            source = operand_rows[side][:, group * GROUP_K : (group + 1) * GROUP_K].rearrange(
                "(n r) (z u k) -> z u r n k", r=BLOCK_ROWS, z=ZONES, u=PAIRS
            )
            for z in range(ZONES):
                for u in range(PAIRS):
                    nc.sync.dma_start(out=raw[unit][BLOCK * z + u : BLOCK * (z + 1) : PAIRS], in_=source[z, u])

        def split(unit, c):
            words[(unit, c)] = split_pool.tile([P, ROWS // BLOCK_ROWS, BLOCK, 2], BF16, name="split", align_bytes=64)
            source = raw[unit][:].rearrange("p n (e q c) -> p c n q e", e=2, q=BLOCK)[:, c]
            if c < BY_GPSIMD:
                for n in range(SPLIT_PIECES):
                    rows = slice(n * 16 // SPLIT_PIECES, (n + 1) * 16 // SPLIT_PIECES)
                    nc.gpsimd.tensor_scalar(out=words[(unit, c)][:, rows], in0=source[:, rows], scalar1=1.0, scalar2=0.0, op0=MULT, op1=ADD)
            else:
                nc.vector.tensor_copy(out=words[(unit, c)][:], in_=source)

        def turn(unit, c):
            if c == 0:
                grouped[unit] = turned_pool.tile([P, COMPS, ROWS, PACK], BF16, name="turned", align_bytes=64)
            nc.vector.transpose(
                grouped[unit][:, c].rearrange("p n t -> p (n t)").bitcast(F32),
                words[(unit, c)][:].rearrange("p n q e -> p (n q e)").bitcast(F32),
            )

        def load(unit):
            if unit >= TURNED_FROM:
                load_turned(unit)
                return
            group, side = divmod(unit, 2)
            for r in range(ROW_TILES):
                raw[(unit, r)] = raw_pool.tile([P, GROUP_K], BF16, name="raw")
                parts = pieces_of(unit)
                for n in range(parts):
                    cols = slice(n * GROUP_K // parts, (n + 1) * GROUP_K // parts)
                    nc.sync.dma_start(
                        out=raw[(unit, r)][:, cols],
                        in_=operand_rows[side][r * P : (r + 1) * P, group * GROUP_K + cols.start : group * GROUP_K + cols.stop],
                    )

        def sort_words(unit):
            for r in range(ROW_TILES):
                words[(unit, r)] = words_pool.tile([P, HALVES, PACK, ZONES, RUN], F32, name="words")
                source = raw[(unit, r)][:].bitcast(F32).rearrange("p (g t q h) -> p h t g q", g=ZONES, t=PACK, q=RUN, h=HALVES)
                parts = pieces_of(unit)
                for n in range(parts):
                    zones = slice(n * ZONES // parts, (n + 1) * ZONES // parts)
                    (nc.gpsimd if (unit, r) in ON_GPSIMD else nc.vector).tensor_copy(
                        out=words[(unit, r)][:, :, :, zones], in_=source[:, :, :, zones]
                    )

        def transpose(unit):
            for r, h in BANK_ORDER if unit else [(r, h) for r in range(ROW_TILES) for h in range(HALVES)]:
                if True:
                    turned[(unit, r, h)] = banks.tile([P, PACK, P], F32, name="bank")
                    for t in range(PACK):
                        nc.tensor.transpose(
                            turned[(unit, r, h)][:, t, :],
                            words[(unit, r)][:, h, t].rearrange("p g q -> p (g q)"),
                            identity[:],
                        )

        def regroup(unit):
            grouped[unit] = grouped_pool.tile([P, COMPS, ROWS, PACK], BF16, name="grouped", align_bytes=64)
            for r, h in BANK_ORDER if unit else [(r, h) for r in range(ROW_TILES) for h in range(HALVES)]:
                if True:
                    pairs = turned[(unit, r, h)][:].bitcast(BF16).rearrange("p t (n e) -> p e n t", e=2)
                    target = grouped[unit][:, 2 * h : 2 * h + 2, r * P : (r + 1) * P, :]
                    if (r, h) == V_BANK and unit not in S_UNITS:
                        nc.vector.tensor_copy(out=target, in_=pairs)
                    else:
                        nc.scalar.copy(out=target, in_=pairs)

        def quantise(unit, parts=(0, 1)):
            group, side = divmod(unit, 2)
            if parts == (0, 1):
                cols = slice(0, COMPS * ROWS)
                source = grouped[unit][:]
            else:
                cols = slice(parts[0] * 2 * ROWS, (parts[0] + 1) * 2 * ROWS)
                source = grouped[unit][:, 2 * parts[0] : 2 * parts[0] + 2]
            nc.vector.quantize_mx(
                out=codes[side][group][:, cols].bitcast(FP8X4),
                scales=scales[side][group][:, cols],
                in_=source.rearrange("p c n t -> p (c n t)"),
            )

        def one_pass(acc, group, bt, c, d, start, stop):
            x_cols = slice(c * ROWS + bt * P, c * ROWS + (bt + 1) * P)
            w_cols = slice((d ^ c) * ROWS, ((d ^ c) + 1) * ROWS)
            nc.tensor.matmul_mx(
                out=acc,
                lhsT=codes[0][group][:, x_cols].bitcast(FP8X4),
                lhsT_scale=scales[0][group][:, x_cols],
                rhs=codes[1][group][:, w_cols].bitcast(FP8X4),
                rhs_scale=scales[1][group][:, w_cols],
                start=start,
                stop=stop,
            )

        def multiply_main(half, d):
            group, bt = divmod(half, ROW_TILES)
            terms = [c for c in range(COMPS) if SIGN[d][c] == MAJORITY[d]]
            for n, c in enumerate(terms):
                one_pass(
                    main[bt][d // 2][:, (d % 2) * ROWS : (d % 2 + 1) * ROWS],
                    group,
                    bt,
                    c,
                    d,
                    start=(group == 0 and d % 2 == 0 and n == 0),
                    stop=(group == GROUPS - 1 and d % 2 == 1 and n == len(terms) - 1),
                )

        def multiply_odd(acc, bt, j, groups, start, stop):
            terms = [(g, c, d) for g in groups for d in (2 * j, 2 * j + 1) for c in range(COMPS) if SIGN[d][c] != MAJORITY[d]]
            for n, (group, c, d) in enumerate(terms):
                one_pass(
                    acc[:, (d % 2) * ROWS : (d % 2 + 1) * ROWS],
                    group,
                    bt,
                    c,
                    d,
                    start=(start and n == 0),
                    stop=(stop and n == len(terms) - 1),
                )

        def combine(out, ins, acc, j):
            if j == 0:
                for d in (0, 1):
                    cols = slice(d * ROWS, (d + 1) * ROWS)
                    nc.vector.tensor_tensor(out=out[:, cols], in0=ins[:, cols], in1=acc[:, cols], op=SUBTRACT if MAJORITY[d] > 0 else ADD)
            else:
                nc.vector.tensor_tensor(out=out, in0=ins, in1=acc, op=SUBTRACT)

        def load_bias():
            nc.sync.dma_start(out=bias_rows[:], in_=B.rearrange("o d -> (o d)").partition_broadcast(P))
            for d in range(COMPS):
                nc.gpsimd.tensor_scalar(
                    out=bias[:, d, :],
                    in0=bias_rows[:].rearrange("p (o d) -> p d o", d=COMPS)[:, d, :],
                    scalar1=1.0,
                    scalar2=0.0,
                    op0=MULT,
                    op1=ADD,
                )

        bias_rows = const.tile([P, ROWS * COMPS], BF16)
        bias = const.tile([P, COMPS, ROWS], F32)
        early_odd = {}

        for unit in range(LOAD_AHEAD):
            load(unit)
        for unit in range(SORT_AHEAD):
            sort_words(unit)
        waiting = []
        odd_items = [(bt, j) for bt in range(ROW_TILES) for j in range(2)]
        splits = [(u, c) for u in range(TURNED_FROM, UNITS) for c in range(COMPS)]
        turns = list(splits)
        done_early = []
        for step in range(TURNED_FROM):
            if step + LOAD_AHEAD < TURNED_FROM:
                load(step + LOAD_AHEAD)
            if step in TURN_LOADS:
                load_turned(TURNED_FROM + TURN_LOADS.index(step))
            if step == 11:
                load_bias()
            transpose(step)
            for stage in V_ORDER if step >= HEAD else V_HEAD:
                if stage == "Q" and step >= 1:
                    quantise(step - 1, (1,) if step - 1 >= SPLIT_FROM and step - 1 < SPLIT_TO else (0, 1))
                    if step % 2 == 0:
                        waiting += [(step - 2 + bt, d) for bt in range(ROW_TILES) for d in range(COMPS)]
                if stage == "X":
                    regroup(step)
                if stage == "A" and SPLIT_FROM <= step < SPLIT_TO:
                    quantise(step, (0,))
                if stage == "T" and step in TURN_STEPS:
                    for u, c in turns[:TURN_QUOTA]:
                        if c == 0 and u > TURNED_FROM:
                            quantise(u - 1)
                            done_early.append(u - 1)
                        turn(u, c)
                    turns = turns[TURN_QUOTA:]
                if stage == "P" and step in SPLIT_STEPS:
                    for u, c in splits[:SPLIT_QUOTA]:
                        split(u, c)
                    splits = splits[SPLIT_QUOTA:]
                if stage == "S" and step + SORT_AHEAD < TURNED_FROM:
                    sort_words(step + SORT_AHEAD)
            quota = QUOTAS[min(step, len(QUOTAS) - 1)]
            quota = min(quota, max(0, len(waiting) - HOLDS[min(step, len(HOLDS) - 1)]))
            for half, d in waiting[:quota]:
                multiply_main(half, d)
            waiting = waiting[quota:]
            if step in ODD_STEPS and odd_items:
                bt, j = odd_items.pop(0)
                odd = banks.tile([P, BANK], F32, name="bank")
                multiply_odd(odd, bt, j, range(ODD_SPLIT), True, True)
                early_odd[(bt, j)] = last.tile([P, BANK], F32, name="early_odd%d%d" % (bt, j), bufs=1)
                (nc.scalar.copy if ODD_ON_SCALAR else nc.vector.tensor_copy)(out=early_odd[(bt, j)][:], in_=odd[:])

        if TURNED_FROM % 2:
            quantise(TURNED_FROM - 1)
        else:
            quantise(TURNED_FROM - 1)
            if TURNED_FROM < UNITS:
                waiting += [(TURNED_FROM - 2 + bt, d) for bt in range(ROW_TILES) for d in range(COMPS)]
        for u in range(TURNED_FROM, UNITS):
            for c in range(COMPS):
                if (u, c) in splits:
                    split(u, c)
            for c in range(COMPS):
                if (u, c) in turns:
                    if c == 0 and u > TURNED_FROM and u - 1 not in done_early:
                        quantise(u - 1)
                        done_early.append(u - 1)
                    turn(u, c)
        for u in range(TURNED_FROM, UNITS):
            if u not in done_early:
                quantise(u)
        for half, d in waiting:
            multiply_main(half, d)
        odds = {}
        for bt in range(ROW_TILES):
            for j in range(2):
                odds[(bt, j)] = banks.tile([P, BANK], F32, name="bank")
                multiply_odd(odds[(bt, j)], bt, j, range(ODD_SPLIT, GROUPS - 1), True, False)
                rest = early_odd[(bt, j)][:]
                combine(rest, bias[:, 2 * j : 2 * j + 2, :].rearrange("p d o -> p (d o)"), rest, j)
        for bt in range(ROW_TILES):
            for j in range(2):
                multiply_odd(odds[(bt, j)], bt, j, (GROUPS - 1,), False, True)
                rest = early_odd[(bt, j)][:]
                combine(rest, rest, odds[(bt, j)][:], j)
            for d in range(COMPS):
                multiply_main(2 * (GROUPS - 1) + bt, d)
            total = last.tile([P, COMPS, ROWS], F32, name="total")
            for d in (0, 1):
                nc.vector.tensor_tensor(
                    out=total[:, d, :],
                    in0=early_odd[(bt, 0)][:, d * ROWS : (d + 1) * ROWS],
                    in1=main[bt][0][:, d * ROWS : (d + 1) * ROWS],
                    op=ADD if MAJORITY[d] > 0 else SUBTRACT,
                )
            result = last.tile([P, ROWS, COMPS], F32, name="result")
            parts = TAIL_PIECES[bt]
            for o_part in range(parts):
                o_cols = slice(o_part * ROWS // parts, (o_part + 1) * ROWS // parts)
                nc.vector.tensor_tensor(
                    out=total[:, 2:4, o_cols],
                    in0=early_odd[(bt, 1)][:].rearrange("p (d o) -> p d o", d=2)[:, :, o_cols],
                    in1=main[bt][1][:].rearrange("p (d o) -> p d o", d=2)[:, :, o_cols],
                    op=ADD,
                )
                nc.scalar.activation(
                    out=result[:, o_cols, :],
                    in_=total[:, :, o_cols].rearrange("p d o -> p o d"),
                    func=mybir.ActivationFunctionType.Tanh,
                )
                nc.sync.dma_start(
                    out=out_rows[bt * P : (bt + 1) * P, o_cols.start * COMPS : o_cols.stop * COMPS],
                    in_=result[:, o_cols, :].rearrange("p o d -> p (o d)"),
                )
